import numpy as np
import ml_dtypes


def mxq(x, axis, fmt="e4m3"):
    dtype, down = {"e4m3": (ml_dtypes.float8_e4m3fn, 7), "e5m2": (ml_dtypes.float8_e5m2, 14)}[fmt]
    v = np.moveaxis(np.asarray(x, np.float32).astype(ml_dtypes.bfloat16).astype(np.float64), axis, -1)
    blocks = v.reshape(v.shape[:-1] + (-1, 32))
    amax = np.abs(blocks).max(-1, keepdims=True)
    byte = np.maximum(np.where(amax > 0, np.frexp(amax)[1] - 1 + 127, 0) - down, 1)
    scale = np.exp2(byte - 127.0)
    codes = (blocks / scale).astype(np.float32).astype(dtype).astype(np.float64)
    return np.moveaxis((codes * scale).reshape(v.shape), -1, axis)


WIDE = False


def mx_kscale(k):
    if not WIDE:
        return np.ones(k)
    levels = np.array([10, -10, 5, -5, 0])
    if k % 512:
        return np.exp2(np.random.permutation(np.resize(levels, k // 32))).repeat(32)
    a = np.empty((k // 512, 16))
    for p in range(k // 512):
        a[p, :8] = np.random.permutation(np.resize(levels, 8))
        for g in range(8):
            far = levels[np.abs(levels - a[p, g]) >= 10]
            a[p, g + 8] = far[np.random.randint(len(far))]
    return np.exp2(a.ravel()).repeat(32)


BF16 = ml_dtypes.bfloat16


def bf(x):
    return np.asarray(x, np.float32).astype(BF16)


def f64(x):
    return np.asarray(x).astype(np.float64)


B, T, C_IN, HIDDEN, HEADS, OUT_DIM = 2, 1024, 1024, 1024, 8, 1024
RMS_EPS = 1.1920928955078125e-07


def silu(z):
    return z / (1.0 + np.exp(-z))


def setup_inputs():
    s, t = mx_kscale(C_IN), mx_kscale(HIDDEN)
    r = np.exp2(-12.0 * np.random.random((B, T, 1)))
    return {"x": bf(np.random.standard_normal((B, T, C_IN)) * s),
            "h_attn": bf(np.random.standard_normal((B, T, HIDDEN)) * 0.8 * r),
            "Wu": bf(np.random.standard_normal((HIDDEN, C_IN)) / np.sqrt(C_IN) / s),
            "bu": bf(np.random.standard_normal(HIDDEN) * 0.1),
            "g_norm": bf((1.0 + 0.1 * np.random.standard_normal(HIDDEN)) * t),
            "Wf": bf(np.random.standard_normal((OUT_DIM, HIDDEN)) / np.sqrt(HIDDEN) / t),
            "b_out": bf(np.random.standard_normal(OUT_DIM) * 0.1)}


def reference(x, h_attn, Wu, bu, g_norm, Wf, b_out):
    u = silu((mxq(f64(x), 2, "e4m3") @ mxq(f64(Wu), 1, "e4m3").T) + f64(bu))
    av = f64(h_attn)
    av_norm = av * (1.0 / np.sqrt(np.mean(av * av, axis=-1, keepdims=True) + RMS_EPS)) * f64(g_norm)
    uv = av_norm * u
    return (mxq(uv, 2, "e4m3") @ mxq(f64(Wf), 1, "e4m3").T) + f64(b_out)

from contextlib import ExitStack

import concourse.mybir as mybir
from concourse.masks import make_identity

F32 = mybir.dt.float32
BF16 = mybir.dt.bfloat16
U32 = mybir.dt.uint32
U8 = mybir.dt.uint8
FP8X4 = mybir.dt.float8_e4m3fn_x4
ACT = mybir.ActivationFunctionType
ALU = mybir.AluOpType

P = 128
PACK = 4
K = 1024
PASSES = K // (P * PACK)
TOKENS = 2048
OUT_DIM = 1024
GROUP = 512
TILES = GROUP // P
CHUNKS = TOKENS // GROUP
HALVES = OUT_DIM // GROUP
TOKEN_TILES = TOKENS // P
HIDDEN_TILES = K // P
PAIRS = HIDDEN_TILES // 2
ROUNDS = CHUNKS * PAIRS
WEIGHT_BLOCKS = PASSES + HALVES
WEIGHT_PAIRS = 2 * WEIGHT_BLOCKS
X_TURN = 6
X_PACK = 5
H_SQUARE = 6
H_SCALE = 5
W_AHEAD = 4
WARM_UP = 6
LAG = 6
TOKEN_RUN = 4
RMS_EPS = 1.1920928955078125e-07

FLOPS = 2 * TOKENS * K * K + 2 * TOKENS * K * OUT_DIM


def within(index, count):
    return 0 <= index < count


def tile_hstu_pb_kernel(tc, x, h_attn, Wu, bu, g_norm, Wf, b_out, out):
    nc = tc.nc

    x_rows = x.flatten_outer_dims().rearrange("(c p i) k -> c i p k", p=P, i=TILES)
    h_rows = h_attn.flatten_outer_dims().rearrange("(c p i) k -> c i p k", p=P, i=TILES)
    out_rows = out.flatten_outer_dims().rearrange("(c p i) o -> c i p o", p=P, i=TILES)
    wu_rows = Wu.rearrange("(g p v b) k -> g v p (b k)", g=PASSES, p=P, v=2, b=2)
    wf_rows = Wf.rearrange("(h v b p) k -> h v p b k", h=HALVES, v=2, b=2, p=P)

    with ExitStack() as stack:

        def open_pool(name, bufs):
            return stack.enter_context(tc.tile_pool(name=name, bufs=bufs))

        keep = open_pool("keep", 1)
        grouped_pool = open_pool("grouped", 8)
        x_pool = open_pool("xcodes", 2)
        norm_pool = open_pool("norm", 2)
        stats_pool = open_pool("stats", 6)
        silu_pool = open_pool("silu", 4)
        gate_pool = open_pool("gate", 2)
        result_pool = open_pool("result", 3)
        psum = stack.enter_context(tc.psum_pool(name="psum", bufs=4))
        stack.enter_context(tc.manual_schedule())

        ident = keep.tile([P, P], F32)
        make_identity(nc, ident[:])
        minus_half = keep.tile([P, 1], F32)
        nc.gpsimd.memset(minus_half[:], -0.5)
        bu_sb = keep.tile([P, HIDDEN_TILES], BF16)
        nc.scalar.dma_start(
            out=bu_sb[:].rearrange("p (g t) -> p g t", t=PACK), in_=bu.rearrange("(g p t) -> p g t", p=P, t=PACK)
        )
        g_sb = keep.tile([P, HIDDEN_TILES], BF16)
        nc.scalar.dma_start(
            out=g_sb[:].rearrange("p (g t) -> p g t", t=PACK), in_=g_norm.rearrange("(g p t) -> p g t", p=P, t=PACK)
        )
        table_warm = keep.tile([P, 1], F32)
        nc.scalar.activation(out=table_warm[:], in_=minus_half[:], func=ACT.Silu)

        x_sb = [keep.tile([P, TILES * K], BF16, name="x%d" % c) for c in range(CHUNKS)]
        h_sb = [keep.tile([P, TILES * K], BF16, name="h%d" % c) for c in range(CHUNKS)]
        w_sb = [keep.tile([P, TILES * K], BF16, name="w%d" % block) for block in range(WEIGHT_BLOCKS)]
        b_out_sb = keep.tile([P, OUT_DIM], BF16)

        def tile_of(rows, i):
            return rows[:, i * K : (i + 1) * K]

        for r in range(-WARM_UP, ROUNDS):
            if within(r + H_SQUARE, TOKEN_TILES):
                c, i = divmod(r + H_SQUARE, TILES)
                nc.sync.dma_start(out=tile_of(h_sb[c], i), in_=h_rows[c][i])
            if within(r + X_TURN, TOKEN_TILES):
                c, i = divmod(r + X_TURN, TILES)
                nc.sync.dma_start(out=tile_of(x_sb[c], i), in_=x_rows[c][i])
            if within(r + W_AHEAD, WEIGHT_PAIRS):
                block, v = divmod(r + W_AHEAD, 2)
                both = w_sb[block][:, 2 * v * K : (2 * v + 2) * K]
                if block < PASSES:
                    nc.sync.dma_start(out=both, in_=wu_rows[block][v])
                else:
                    nc.sync.dma_start(out=both.rearrange("p (b k) -> p b k", b=2), in_=wf_rows[block - PASSES][v])
            if r + W_AHEAD == WEIGHT_PAIRS:
                nc.sync.dma_start(out=b_out_sb[:], in_=b_out.partition_broadcast(P))

        def codes_and_scales(pool, name):
            codes = pool.tile([P, PASSES * GROUP], U32, name=name + "_codes", align_bytes=64)
            scales = pool.tile([P, PASSES * GROUP], U8, name=name + "_scales", align_bytes=64)
            return codes, scales

        def turn(rows, b, ring):
            words = rows[:].bitcast(F32)
            turned = psum.tile([P, PASSES, 2, P], F32, name="turned", tag=ring)
            for g in range(PASSES):
                for u in range(2):
                    first = b * (K // 2) + 2 * g * P
                    nc.tensor.transpose(turned[:, g, u, :], words[:, first + u : first + 2 * P : 2], ident[:])
            return turned

        def spread(copy, turned):
            grouped = grouped_pool.tile([P, PASSES * P * PACK], BF16, name="grouped", align_bytes=64)
            copy(
                out=grouped[:].bitcast(F32).rearrange("p (g r u) -> p g r u", g=PASSES, u=2),
                in_=turned[:].rearrange("p g u r -> p g r u"),
            )
            return grouped

        def pack(grouped, operand, b):
            codes, scales = operand
            for g in range(PASSES):
                cols = slice(g * GROUP + b * P, g * GROUP + (b + 1) * P)
                nc.vector.quantize_mx(
                    out=codes[:, cols].bitcast(FP8X4),
                    scales=scales[:, cols],
                    in_=grouped[:, g * P * PACK : (g + 1) * P * PACK],
                )

        def mx_product(stationary, m_tile, moving):
            bank = psum.tile([P, GROUP], F32, name="acc", tag="mx")
            for g in range(PASSES):
                m_cols = slice(g * GROUP + m_tile * P, g * GROUP + (m_tile + 1) * P)
                n_cols = slice(g * GROUP, (g + 1) * GROUP)
                nc.tensor.matmul_mx(
                    out=bank[:],
                    lhsT=stationary[0][:, m_cols].bitcast(FP8X4),
                    lhsT_scale=stationary[1][:, m_cols],
                    rhs=moving[0][:, n_cols].bitcast(FP8X4),
                    rhs_scale=moving[1][:, n_cols],
                    start=(g == 0),
                    stop=(g == PASSES - 1),
                )
            return bank

        def inverse_rms(t):
            squares = norm_pool.tile([P, K], BF16, name="squares")
            mean_sq = stats_pool.tile([P, 1], F32, name="mean_sq")
            nc.scalar.activation(
                out=squares[:],
                in_=tile_of(h_sb[t // TILES], t % TILES),
                func=ACT.Square,
                scale=K**-0.5,
                accum_out=mean_sq[:],
            )
            shifted = stats_pool.tile([P, 1], F32, name="shifted")
            nc.gpsimd.tensor_scalar(
                out=shifted[:], in0=mean_sq[:], scalar1=1.0, scalar2=RMS_EPS, op0=ALU.mult, op1=ALU.add
            )
            rstd = stats_pool.tile([P, 1], F32, name="rstd")
            nc.gpsimd.tensor_tensor(out=rstd[:], in0=shifted[:], in1=minus_half[:], op=ALU.pow)
            return rstd

        def sorted_half(t, half):
            sorted_out = h_norm_of[t // TILES][:, t % TILES, :].rearrange("p (g t m) -> p g t m", t=PACK, m=P)
            sorted_in = tile_of(h_sb[t // TILES], t % TILES).rearrange("p (g m t) -> p g t m", m=P, t=PACK)
            return sorted_out[:, half], sorted_in[:, half]

        def normalise(engine, t, half):
            sorted_out, sorted_in = sorted_half(t, half)
            engine.tensor_scalar(
                out=sorted_out, in0=sorted_in, scalar1=rstd_of[t][:], scalar2=0.0, op0=ALU.mult, op1=ALU.add
            )

        def normalise_on_scalar(t, half):
            sorted_out, sorted_in = sorted_half(t, half)
            nc.scalar.activation(out=sorted_out, in_=sorted_in, func=ACT.Copy, scale=rstd_of[t][:])

        w_q = [codes_and_scales(keep, "w%d" % block) for block in range(WEIGHT_BLOCKS)]
        x_q = {}
        uv_q = {}
        h_norm_of = {}
        planes = {}
        x_grouped = {}
        rstd_of = {}

        for r in range(-WARM_UP, ROUNDS + LAG):
            chunk, pair = divmod(r, PAIRS)
            hidden = [2 * pair, 2 * pair + 1] if within(r, ROUNDS) else []
            g2 = pair // 2
            behind = r - LAG
            x_new = r + X_TURN
            x_ready = r + X_PACK
            h_new = r + H_SQUARE
            h_ready = r + H_SCALE
            w_new = r + W_AHEAD
            early = x_new < TILES

            z = [mx_product(w_q[g2], j % PACK, x_q[chunk]) for j in hidden]
            projected = []
            if within(behind, TOKEN_TILES):
                projected = [
                    mx_product(uv_q[behind // TILES], behind % TILES, w_q[PASSES + h]) for h in range(HALVES)
                ]

            h_turned = []
            for j in hidden:
                h_turned.append(psum.tile([P, GROUP], F32, name="h_turned", tag="turn"))
                for i in range(TILES):
                    nc.tensor.transpose(
                        h_turned[-1][:, i * P : (i + 1) * P], h_norm_of[chunk][:, i, j * P : (j + 1) * P], ident[:]
                    )
            if within(x_new, TOKEN_TILES):
                x_turned = turn(x_sb[x_new // TILES], x_new % TILES, "turn")
            w_turned = []
            if within(w_new, WEIGHT_PAIRS):
                w_tiles = [2 * (w_new % 2), 2 * (w_new % 2) + 1]
                w_turned = [turn(w_sb[w_new // 2], b, "mx") for b in w_tiles]

            u = []
            for s, j in enumerate(hidden):
                u.append(silu_pool.tile([P, GROUP], F32, name="u"))
                nc.scalar.activation(out=u[s][:], in_=z[s][:], func=ACT.Silu, bias=bu_sb[:, j : j + 1], scale=1.0)
            if within(h_new, TOKEN_TILES):
                rstd_of[h_new] = inverse_rms(h_new)
            if within(x_new, TOKEN_TILES) and not early:
                x_grouped[x_new] = spread(nc.scalar.copy, x_turned)
            w_grouped = [spread(nc.scalar.copy, w_turned[0])] if w_turned and r < 0 else []

            if within(h_ready, TOKEN_TILES):
                if h_ready % TILES == 0:
                    h_norm_of[h_ready // TILES] = norm_pool.tile([P, TILES, K], F32, name="h_norm")
                if h_ready >= TILES:
                    normalise(nc.gpsimd, h_ready, 0)
                    normalise_on_scalar(h_ready, 1)

            if projected:
                result = result_pool.tile([P, OUT_DIM], F32, name="result")
                for h in range(HALVES):
                    o_cols = slice(h * GROUP, (h + 1) * GROUP)
                    nc.vector.tensor_tensor(
                        out=result[:, o_cols], in0=projected[h][:], in1=b_out_sb[:, o_cols], op=ALU.add
                    )
                    nc.sync.dma_start(out=out_rows[behind // TILES][behind % TILES][:, o_cols], in_=result[:, o_cols])
            if hidden and pair % 2 == 0:
                planes[g2] = gate_pool.tile([P, PACK, GROUP], BF16, name="planes")
            for s, j in enumerate(hidden):
                nc.vector.scalar_tensor_tensor(
                    out=planes[g2][:, j % PACK, :],
                    in0=h_turned[s][:],
                    scalar=g_sb[:, j : j + 1],
                    in1=u[s][:],
                    op0=ALU.mult,
                    op1=ALU.mult,
                )
            if within(x_new, TOKEN_TILES) and early:
                x_grouped[x_new] = spread(nc.vector.tensor_copy, x_turned)
            for turned in w_turned[len(w_grouped) :]:
                w_grouped.append(spread(nc.vector.tensor_copy, turned))
            if within(h_ready, TILES):
                normalise(nc.vector, h_ready, 0)
                normalise(nc.vector, h_ready, 1)
            if within(x_ready, TOKEN_TILES):
                if x_ready % TILES == 0:
                    x_q[x_ready // TILES] = codes_and_scales(x_pool, "x")
                pack(x_grouped[x_ready], x_q[x_ready // TILES], x_ready % TILES)
            for s in range(len(w_turned)):
                pack(w_grouped[s], w_q[w_new // 2], w_tiles[s])
            if within(r - 1, ROUNDS) and pair % 2 == 0:
                done_chunk, done_pair = divmod(r - 1, PAIRS)
                done_pass = done_pair // 2
                if done_pass == 0:
                    uv_q[done_chunk] = codes_and_scales(gate_pool, "uv")
                cols = slice(done_pass * GROUP, (done_pass + 1) * GROUP)
                nc.vector.quantize_mx(
                    out=uv_q[done_chunk][0][:, cols].bitcast(FP8X4),
                    scales=uv_q[done_chunk][1][:, cols],
                    in_=uv_grouped[:].rearrange("p r t -> p (r t)"),
                )
            if hidden and pair % 2 == 1:
                uv_grouped = gate_pool.tile([P, GROUP, PACK], BF16, name="uv_grouped", align_bytes=64)
                nc.vector.tensor_copy(
                    out=uv_grouped[:].rearrange("p (n i) t -> p n t i", i=TOKEN_RUN),
                    in_=planes[g2][:].rearrange("p t (n i) -> p n t i", i=TOKEN_RUN),
                )
